import numpy as np
import ml_dtypes


def mxq(x, axis, fmt="e4m3"):
    dtype, down = {"e4m3": (ml_dtypes.float8_e4m3fn, 7), "e5m2": (ml_dtypes.float8_e5m2, 14)}[fmt]
    v = np.moveaxis(np.asarray(x, np.float32).astype(ml_dtypes.bfloat16).astype(np.float64), axis, -1)
    blocks = v.reshape(v.shape[:-1] + (-1, 32))
    amax = np.abs(blocks).max(-1, keepdims=True)
    byte = np.maximum(np.where(amax > 0, np.frexp(amax)[1] - 1 + 127, 0) - down, 1)
    scale = np.exp2(byte - 127.0)
    codes = (blocks / scale).astype(np.float32).astype(dtype).astype(np.float64)
    return np.moveaxis((codes * scale).reshape(v.shape), -1, axis)


WIDE = False


def mx_kscale(k):
    if not WIDE:
        return np.ones(k)
    levels = np.array([10, -10, 5, -5, 0])
    if k % 512:
        return np.exp2(np.random.permutation(np.resize(levels, k // 32))).repeat(32)
    a = np.empty((k // 512, 16))
    for p in range(k // 512):
        a[p, :8] = np.random.permutation(np.resize(levels, 8))
        for g in range(8):
            far = levels[np.abs(levels - a[p, g]) >= 10]
            a[p, g + 8] = far[np.random.randint(len(far))]
    return np.exp2(a.ravel()).repeat(32)


BF16 = ml_dtypes.bfloat16


def bf(x):
    return np.asarray(x, np.float32).astype(BF16)


def f64(x):
    return np.asarray(x).astype(np.float64)


T, B, D, M = 128, 32, 1024, 512
TEMP = 0.1
QS = 0.3
SC = 2.0
MS = SC * TEMP / (QS * np.sqrt(D))
WS = QS * np.sqrt(SC**2 / D + 0.4 / B)


def sigmoid(v):
    return 1.0 / (1.0 + np.exp(-v))


def setup_inputs():
    s = mx_kscale(D)
    return {"queries": bf(np.random.standard_normal((T, B, D)) * QS / s),
            "memory_items": bf(np.random.standard_normal((M, D)) * MS * s),
            "wq": bf(np.random.standard_normal((M, D)) * WS * s),
            "U_w": bf(np.random.standard_normal((D, D)) / (MS * np.sqrt(D)) / s[None, :]),
            "W_w": bf(np.random.standard_normal((D, D)) / (WS * np.sqrt(D)) / s[None, :])}


def reference(queries, memory_items, wq, U_w, W_w):
    q = f64(queries).reshape(T * B, D)
    mem = f64(memory_items)
    w = f64(wq)
    gate = sigmoid((mxq(mem, 1, "e4m3") @ mxq(f64(U_w), 1, "e4m3").T) + (mxq(w, 1, "e4m3") @ mxq(f64(W_w), 1, "e4m3").T))
    m_new = (1.0 - gate) * mem + gate * w
    logits = (mxq(q, 1, "e4m3") @ mxq(m_new, 1, "e4m3").T) / TEMP
    e = np.exp(logits - logits.max(-1, keepdims=True))
    w_att = e / e.sum(-1, keepdims=True)
    return m_new, w_att.reshape(T, B, M)

@@ -1,0 +1,368 @@
+from contextlib import ExitStack
+
+import concourse.mybir as mybir
+from concourse.masks import make_identity
+
+F32 = mybir.dt.float32
+BF16 = mybir.dt.bfloat16
+U32 = mybir.dt.uint32
+U8 = mybir.dt.uint8
+FP8X4 = mybir.dt.float8_e4m3fn_x4
+ACT = mybir.ActivationFunctionType
+ALU = mybir.AluOpType
+
+P = 128
+FEATURES = 1024
+SLOTS = 512
+BATCH = 32
+TEMPERATURE = 0.1
+PACK = 4
+K_PASS = P * PACK
+PASSES = FEATURES // K_PASS
+TILES = 4
+CHUNK_ROWS = TILES * P
+CHUNK_WORDS = CHUNK_ROWS * PASSES
+HALVES = FEATURES // CHUNK_ROWS
+QUERY_CHUNKS = BATCH // TILES
+QUERY_BUFFERS = 4
+STORE_TILES = 2
+
+FLOPS = 2 * (2 * SLOTS * FEATURES * FEATURES) + 2 * (P * BATCH) * SLOTS * FEATURES
+
+
+def stationary_cols(n, g):
+    return slice((n * PASSES + g) * P, (n * PASSES + g + 1) * P)
+
+
+def moving_cols(g):
+    return slice(g * CHUNK_ROWS, (g + 1) * CHUNK_ROWS)
+
+
+def in_tile_order(bank):
+    return bank.rearrange("p (n r) -> p r n", n=TILES)
+
+
+def in_row_order(row):
+    return row.rearrange("p (r n) -> p r n", n=TILES)
+
+
+def tile_gatedmemorymodule_pb_t_kernel(tc, queries, memory_items, wq, U_w, W_w, out_0, out_1):
+    nc = tc.nc
+    with ExitStack() as ctx:
+        keep = ctx.enter_context(tc.tile_pool(name="keep", bufs=1))
+        weight_rows = ctx.enter_context(tc.tile_pool(name="weight_rows", bufs=2 * HALVES))
+        query_rows = ctx.enter_context(tc.tile_pool(name="query_rows", bufs=QUERY_BUFFERS))
+        regroup = ctx.enter_context(tc.tile_pool(name="regroup", bufs=3))
+        query_mx = ctx.enter_context(tc.tile_pool(name="query_mx", bufs=4))
+        gates = ctx.enter_context(tc.tile_pool(name="gates", bufs=3))
+        answers = ctx.enter_context(tc.tile_pool(name="answers", bufs=3))
+        stats = ctx.enter_context(tc.tile_pool(name="stats", bufs=3))
+        turn_banks = ctx.enter_context(tc.psum_pool(name="turn_banks", bufs=TILES))
+        sum_banks = ctx.enter_context(tc.psum_pool(name="sum_banks", bufs=TILES))
+        ctx.enter_context(tc.manual_schedule())
+
+        identity = keep.tile([P, P], F32)
+        make_identity(nc, identity[:])
+
+        def load_rows(pool, rows, label):
+            raw = pool.tile([P, TILES, FEATURES], BF16, name=label)
+            nc.sync.dma_start(out=raw[:], in_=rows.rearrange("(p n) k -> p n k", n=TILES))
+            return raw
+
+        def load_queries(c):
+            raw = query_rows.tile([P, TILES, FEATURES], BF16, name="query_raw")
+            nc.sync.dma_start(out=raw[:], in_=queries[:, c * TILES : (c + 1) * TILES, :])
+            return raw
+
+        def new_operand(pool, label):
+            codes = pool.tile([P, CHUNK_WORDS], U32, name=label + "_codes", align_bytes=64)
+            scales = pool.tile([P, CHUNK_WORDS], U8, name=label + "_scales", align_bytes=64)
+            return codes, scales
+
+        def input_chunk(raw, operand, order):
+            words = raw[:].bitcast(F32)
+            return {
+                "blocks": [
+                    [words[:, n, 2 * P * g + u : 2 * P * (g + 1) : 2] for g in range(PASSES) for u in range(2)]
+                    for n in range(TILES)
+                ],
+                "order": order,
+                "codes": operand[0][:],
+                "scales": operand[1][:],
+                "banks": [],
+            }
+
+        def slots_chunk(g):
+            blocks = []
+            for n in range(TILES):
+                by_code = new_slots[:, n, g * K_PASS : (g + 1) * K_PASS].rearrange("p (q t) -> p t q", t=PACK)
+                blocks.append([by_code[:, t, :] for t in range(PACK)])
+            return {
+                "blocks": blocks,
+                "order": None,
+                "codes": new_mx[0][:, moving_cols(g)],
+                "scales": new_mx[1][:, moving_cols(g)],
+                "banks": [],
+            }
+
+        def turn(chunk, n):
+            turned = turn_banks.tile([P, PACK, P], F32, tag="turned")
+            for j in range(PACK):
+                nc.tensor.transpose(turned[:, j, :], chunk["blocks"][n][j], identity[:])
+            chunk["banks"].append(turned)
+
+        def make_room(chunk):
+            if chunk["order"] is None:
+                grouped = regroup.tile([P, SLOTS * PACK], BF16, tag="grouped", align_bytes=64)
+                chunk["targets"] = grouped[:].rearrange("p (n g r t) -> p n g r t", n=TILES, g=1, t=PACK)
+                chunk["side_by_side"] = PACK
+            else:
+                grouped = regroup.tile([P, CHUNK_WORDS * PACK], BF16, tag="grouped", align_bytes=64)
+                chunk["targets"] = grouped[:].bitcast(F32).rearrange(
+                    "p (" + chunk["order"] + " u) -> p n g r u", n=TILES, g=PASSES, u=2
+                )
+                chunk["side_by_side"] = 2
+            chunk["grouped"] = grouped
+
+        def copy_out(chunk, n, engine_copy):
+            engine_copy(
+                out=chunk["targets"][:, n],
+                in_=chunk["banks"][n][:].rearrange("p (g u) r -> p g r u", u=chunk["side_by_side"]),
+            )
+
+        def roll(leaving, entering, vector_helps):
+            if leaving is not None:
+                make_room(leaving)
+            for n in range(TILES):
+                if leaving is not None:
+                    if vector_helps and n == TILES - 1:
+                        copy_out(leaving, n, nc.vector.tensor_copy)
+                    else:
+                        copy_out(leaving, n, nc.scalar.copy)
+                if entering is not None:
+                    turn(entering, n)
+
+        def quantise(chunk):
+            nc.vector.quantize_mx(
+                out=chunk["codes"].bitcast(FP8X4), scales=chunk["scales"], in_=chunk["grouped"][:]
+            )
+
+        def products(total, n, slot_mx, weight_mx, first):
+            for g in range(PASSES):
+                nc.tensor.matmul_mx(
+                    out=total[:],
+                    lhsT=slot_mx[0][:, stationary_cols(n, g)].bitcast(FP8X4),
+                    lhsT_scale=slot_mx[1][:, stationary_cols(n, g)],
+                    rhs=weight_mx[0][:, moving_cols(g)].bitcast(FP8X4),
+                    rhs_scale=weight_mx[1][:, moving_cols(g)],
+                    start=(first and g == 0),
+                    stop=(not first and g == PASSES - 1),
+                )
+
+        def blend(h, n, total):
+            cols = slice(h * CHUNK_ROWS, (h + 1) * CHUNK_ROWS)
+            lift = gates.tile([P, CHUNK_ROWS], F32)
+            nc.scalar.activation(out=in_row_order(lift[:]), in_=in_tile_order(total[:]), func=ACT.Tanh, scale=0.5)
+            nc.vector.scalar_tensor_tensor(
+                out=lift[:], in0=lift[:], scalar=1.0, in1=step[:, n, cols], op0=ALU.add, op1=ALU.mult
+            )
+            nc.vector.scalar_tensor_tensor(
+                out=new_slots[:, n, cols], in0=lift[:], scalar=0.5, in1=memory_raw[:, n, cols],
+                op0=ALU.mult, op1=ALU.add,
+            )
+
+        def store_slots(h):
+            cols = slice(h * CHUNK_ROWS, (h + 1) * CHUNK_ROWS)
+            nc.sync.dma_start(
+                out=out_0.rearrange("(p n) k -> p n k", n=TILES)[:, :, cols], in_=new_slots[:, :, cols]
+            )
+
+        query_raw = {}
+        query = {}
+
+        def query_chunk(c):
+            if c >= QUERY_CHUNKS:
+                return None
+            if c not in query:
+                query[c] = input_chunk(query_raw[c], new_operand(query_mx, "query"), "n g r")
+            return query[c]
+
+        def refill(c):
+            if c + QUERY_BUFFERS < QUERY_CHUNKS:
+                query_raw[c + QUERY_BUFFERS] = load_queries(c + QUERY_BUFFERS)
+
+        def begin_answer(c):
+            answer = answers.tile([P, TILES, SLOTS], F32)
+            shift = stats.tile([P, TILES], F32)
+            row_sum = stats.tile([P, TILES], F32)
+            inverse = stats.tile([P, TILES], F32)
+            query[c]["answer"] = answer
+            query[c]["shift"] = shift
+            query[c]["row_sum"] = row_sum
+            query[c]["inverse"] = inverse
+            query[c]["sums"] = []
+
+        def logit_pass(c, n, g):
+            if g == 0:
+                total = sum_banks.tile([P, SLOTS], F32, tag="total")
+                query[c]["sums"].append(total)
+            nc.tensor.matmul_mx(
+                out=query[c]["sums"][n][:],
+                lhsT=query[c]["codes"][:, stationary_cols(n, g)].bitcast(FP8X4),
+                lhsT_scale=query[c]["scales"][:, stationary_cols(n, g)],
+                rhs=new_mx[0][:, moving_cols(g)].bitcast(FP8X4),
+                rhs_scale=new_mx[1][:, moving_cols(g)],
+                start=(g == 0),
+                stop=(g == PASSES - 1),
+            )
+
+        def multiply(c, n):
+            for g in range(PASSES):
+                logit_pass(c, n, g)
+
+        def leave_bank(c, n):
+            nc.vector.tensor_scalar(
+                out=in_row_order(query[c]["answer"][:, n, :]),
+                in0=in_tile_order(query[c]["sums"][n][:]),
+                scalar1=-1.0 / TEMPERATURE,
+                scalar2=None,
+                op0=ALU.mult,
+                op1=ALU.min,
+                accum_out=query[c]["shift"][:, n : n + 1],
+            )
+
+        def exponential(c, n):
+            nc.scalar.activation(
+                out=query[c]["answer"][:, n, :],
+                in_=query[c]["answer"][:, n, :],
+                func=ACT.Exp,
+                bias=query[c]["shift"][:, n : n + 1],
+                scale=-1.0,
+                accum_out=query[c]["row_sum"][:, n : n + 1],
+            )
+
+        def normalise(c):
+            nc.vector.reciprocal(out=query[c]["inverse"][:], in_=query[c]["row_sum"][:])
+            for n in range(TILES):
+                row = query[c]["answer"][:, n, :]
+                factor = query[c]["inverse"][:, n : n + 1]
+                if c == QUERY_CHUNKS - 1:
+                    nc.vector.tensor_scalar_mul(out=row, in0=row, scalar1=factor)
+                else:
+                    nc.gpsimd.tensor_scalar(
+                        out=row, in0=row, scalar1=factor, scalar2=0.0, op0=ALU.mult, op1=ALU.add
+                    )
+                if (n + 1) % STORE_TILES == 0:
+                    done = slice(n + 1 - STORE_TILES, n + 1)
+                    entries = slice(c * TILES + n + 1 - STORE_TILES, c * TILES + n + 1)
+                    nc.sync.dma_start(out=out_1[:, entries, :], in_=query[c]["answer"][:, done, :])
+
+        memory_raw = load_rows(keep, memory_items, "memory_raw")
+        u_raw = [load_rows(weight_rows, U_w[0:CHUNK_ROWS, :], "weight_raw")]
+        pooled_raw = load_rows(keep, wq, "pooled_raw")
+        w_raw = [load_rows(weight_rows, W_w[0:CHUNK_ROWS, :], "weight_raw")]
+        u_raw.append(load_rows(weight_rows, U_w[CHUNK_ROWS:FEATURES, :], "weight_raw"))
+        w_raw.append(load_rows(weight_rows, W_w[CHUNK_ROWS:FEATURES, :], "weight_raw"))
+        for c in range(QUERY_BUFFERS):
+            query_raw[c] = load_queries(c)
+
+        memory_mx = new_operand(keep, "memory")
+        pooled_mx = new_operand(keep, "pooled")
+        u_mx = [new_operand(keep, "u%d" % h) for h in range(HALVES)]
+        w_mx = [new_operand(keep, "w%d" % h) for h in range(HALVES)]
+        new_mx = new_operand(keep, "new_slots")
+        step = keep.tile([P, TILES, FEATURES], F32)
+        new_slots = keep.tile([P, TILES, FEATURES], F32)
+
+        memory_chunk = input_chunk(memory_raw, memory_mx, "n g r")
+        pooled_chunk = input_chunk(pooled_raw, pooled_mx, "n g r")
+        u_chunk = [input_chunk(u_raw[h], u_mx[h], "g n r") for h in range(HALVES)]
+        w_chunk = [input_chunk(w_raw[h], w_mx[h], "g n r") for h in range(HALVES)]
+        new_chunk = [slots_chunk(g) for g in range(PASSES)]
+
+        def difference(n):
+            nc.vector.tensor_sub(out=step[:, n, :], in0=pooled_raw[:, n, :], in1=memory_raw[:, n, :])
+
+        sums = [{}, {}]
+        first_pair = range(0, TILES // 2)
+        second_pair = range(TILES // 2, TILES)
+
+        def start_sums(h, tiles):
+            for n in tiles:
+                total = sum_banks.tile([P, CHUNK_ROWS], F32, tag="total")
+                sums[h][n] = total
+                products(total, n, memory_mx, u_mx[h], True)
+
+        def finish_sums(h, tiles):
+            for n in tiles:
+                products(sums[h][n], n, pooled_mx, w_mx[h], False)
+
+        def blend_tiles(h, tiles):
+            for n in tiles:
+                blend(h, n, sums[h][n])
+
+        roll(None, memory_chunk, False)
+        roll(memory_chunk, u_chunk[0], False)
+        quantise(memory_chunk)
+        roll(u_chunk[0], pooled_chunk, False)
+        quantise(u_chunk[0])
+        start_sums(0, first_pair)
+        roll(pooled_chunk, w_chunk[0], False)
+        quantise(pooled_chunk)
+        difference(0)
+        difference(1)
+        start_sums(0, second_pair)
+        roll(w_chunk[0], u_chunk[1], False)
+        quantise(w_chunk[0])
+        difference(2)
+        difference(3)
+        finish_sums(0, first_pair)
+        roll(u_chunk[1], w_chunk[1], False)
+        quantise(u_chunk[1])
+        blend_tiles(0, first_pair)
+        finish_sums(0, second_pair)
+        roll(w_chunk[1], query_chunk(0), False)
+        refill(0)
+        quantise(w_chunk[1])
+        start_sums(1, first_pair)
+        blend_tiles(0, second_pair)
+        store_slots(0)
+        roll(query_chunk(0), None, False)
+        finish_sums(1, first_pair)
+        start_sums(1, second_pair)
+        finish_sums(1, second_pair)
+        blend_tiles(1, first_pair)
+        roll(None, new_chunk[0], False)
+        blend_tiles(1, second_pair)
+        store_slots(1)
+        quantise(query_chunk(0))
+        roll(new_chunk[0], new_chunk[1], False)
+        quantise(new_chunk[0])
+        begin_answer(0)
+        for n in range(TILES):
+            logit_pass(0, n, 0)
+        roll(new_chunk[1], query_chunk(1), False)
+        refill(1)
+        quantise(new_chunk[1])
+        for n in range(TILES):
+            logit_pass(0, n, 1)
+
+        roll(query_chunk(1), query_chunk(2), False)
+        refill(2)
+        quantise(query_chunk(1))
+        roll(query_chunk(2), query_chunk(3), False)
+        refill(3)
+        for c in range(QUERY_CHUNKS):
+            if c + 1 < QUERY_CHUNKS:
+                begin_answer(c + 1)
+            for n in range(TILES):
+                leave_bank(c, n)
+                if c + 1 < QUERY_CHUNKS:
+                    multiply(c + 1, n)
+                exponential(c, n)
+            if c + 3 < QUERY_CHUNKS:
+                roll(query_chunk(c + 3), query_chunk(c + 4), True)
+                refill(c + 4)
+            if c + 2 < QUERY_CHUNKS:
+                quantise(query_chunk(c + 2))
+            normalise(c)

@@ -24,7 +24,10 @@ CHUNK_ROWS = TILES * P
 CHUNK_WORDS = CHUNK_ROWS * PASSES
 HALVES = FEATURES // CHUNK_ROWS
 QUERY_CHUNKS = BATCH // TILES
-QUERY_BUFFERS = 4
+ROW_BUFFERS = 6
+SORT = {"p": 1, "w0": 1, "u1": 1, "w1": 1}
+ROUND = "V"
+RG = 4
 STORE_TILES = 2
 
 FLOPS = 2 * (2 * SLOTS * FEATURES * FEATURES) + 2 * (P * BATCH) * SLOTS * FEATURES
@@ -50,11 +53,11 @@ def tile_gatedmemorymodule_pb_t_kernel(tc, queries, memory_items, wq, U_w, W_w, 
     nc = tc.nc
     with ExitStack() as ctx:
         keep = ctx.enter_context(tc.tile_pool(name="keep", bufs=1))
-        weight_rows = ctx.enter_context(tc.tile_pool(name="weight_rows", bufs=2 * HALVES))
-        query_rows = ctx.enter_context(tc.tile_pool(name="query_rows", bufs=QUERY_BUFFERS))
-        regroup = ctx.enter_context(tc.tile_pool(name="regroup", bufs=3))
-        query_mx = ctx.enter_context(tc.tile_pool(name="query_mx", bufs=4))
-        gates = ctx.enter_context(tc.tile_pool(name="gates", bufs=3))
+        rows_pool = ctx.enter_context(tc.tile_pool(name="rows_pool", bufs=ROW_BUFFERS))
+        sorted_pool = ctx.enter_context(tc.tile_pool(name="sorted_pool", bufs=6))
+        regroup = ctx.enter_context(tc.tile_pool(name="regroup", bufs=RG))
+        mx_pool = ctx.enter_context(tc.tile_pool(name="mx_pool", bufs=7))
+        gates = ctx.enter_context(tc.tile_pool(name="gates", bufs=4))
         answers = ctx.enter_context(tc.tile_pool(name="answers", bufs=3))
         stats = ctx.enter_context(tc.tile_pool(name="stats", bufs=3))
         turn_banks = ctx.enter_context(tc.psum_pool(name="turn_banks", bufs=TILES))
@@ -64,13 +67,16 @@ def tile_gatedmemorymodule_pb_t_kernel(tc, queries, memory_items, wq, U_w, W_w, 
         identity = keep.tile([P, P], F32)
         make_identity(nc, identity[:])
 
-        def load_rows(pool, rows, label):
+        def load_rows(pool, rows, label, pieces=1):
             raw = pool.tile([P, TILES, FEATURES], BF16, name=label)
-            nc.sync.dma_start(out=raw[:], in_=rows.rearrange("(p n) k -> p n k", n=TILES))
+            view = rows.rearrange("(p n) k -> p n k", n=TILES)
+            for i in range(pieces):
+                part = slice(i * TILES // pieces, (i + 1) * TILES // pieces)
+                nc.sync.dma_start(out=raw[:, part, :], in_=view[:, part, :])
             return raw
 
         def load_queries(c):
-            raw = query_rows.tile([P, TILES, FEATURES], BF16, name="query_raw")
+            raw = rows_pool.tile([P, TILES, FEATURES], BF16, name="rows")
             nc.sync.dma_start(out=raw[:], in_=queries[:, c * TILES : (c + 1) * TILES, :])
             return raw
 
@@ -79,72 +85,52 @@ def tile_gatedmemorymodule_pb_t_kernel(tc, queries, memory_items, wq, U_w, W_w, 
             scales = pool.tile([P, CHUNK_WORDS], U8, name=label + "_scales", align_bytes=64)
             return codes, scales
 
-        def input_chunk(raw, operand, order):
+        def chunk_of(raw, operand, order):
             words = raw[:].bitcast(F32)
             return {
+                "raw": words,
                 "blocks": [
                     [words[:, n, 2 * P * g + u : 2 * P * (g + 1) : 2] for g in range(PASSES) for u in range(2)]
                     for n in range(TILES)
                 ],
                 "order": order,
-                "codes": operand[0][:],
-                "scales": operand[1][:],
-                "banks": [],
+                "operand": operand,
+                "banks": {},
             }
 
-        def slots_chunk(g):
-            blocks = []
-            for n in range(TILES):
-                by_code = new_slots[:, n, g * K_PASS : (g + 1) * K_PASS].rearrange("p (q t) -> p t q", t=PACK)
-                blocks.append([by_code[:, t, :] for t in range(PACK)])
-            return {
-                "blocks": blocks,
-                "order": None,
-                "codes": new_mx[0][:, moving_cols(g)],
-                "scales": new_mx[1][:, moving_cols(g)],
-                "banks": [],
-            }
+        def sort_words(chunk, n, engine_copy):
+            ordered = sorted_pool.tile([P, FEATURES], BF16, tag="ordered")
+            words = ordered[:].bitcast(F32)
+            engine_copy(
+                out=words.rearrange("p (g u q) -> p g u q", g=PASSES, u=2),
+                in_=chunk["raw"][:, n, :].rearrange("p (g q u) -> p g u q", g=PASSES, u=2),
+            )
+            chunk["blocks"][n] = [words[:, j * P : (j + 1) * P] for j in range(PACK)]
 
         def turn(chunk, n):
             turned = turn_banks.tile([P, PACK, P], F32, tag="turned")
             for j in range(PACK):
                 nc.tensor.transpose(turned[:, j, :], chunk["blocks"][n][j], identity[:])
-            chunk["banks"].append(turned)
+            chunk["banks"][n] = turned
 
-        def make_room(chunk):
-            if chunk["order"] is None:
-                grouped = regroup.tile([P, SLOTS * PACK], BF16, tag="grouped", align_bytes=64)
-                chunk["targets"] = grouped[:].rearrange("p (n g r t) -> p n g r t", n=TILES, g=1, t=PACK)
-                chunk["side_by_side"] = PACK
-            else:
+        def copy_out(chunk, n, engine_copy):
+            if "grouped" not in chunk:
                 grouped = regroup.tile([P, CHUNK_WORDS * PACK], BF16, tag="grouped", align_bytes=64)
+                chunk["grouped"] = grouped
                 chunk["targets"] = grouped[:].bitcast(F32).rearrange(
                     "p (" + chunk["order"] + " u) -> p n g r u", n=TILES, g=PASSES, u=2
                 )
-                chunk["side_by_side"] = 2
-            chunk["grouped"] = grouped
-
-        def copy_out(chunk, n, engine_copy):
             engine_copy(
                 out=chunk["targets"][:, n],
-                in_=chunk["banks"][n][:].rearrange("p (g u) r -> p g r u", u=chunk["side_by_side"]),
+                in_=chunk["banks"][n][:].rearrange("p (g u) r -> p g r u", u=2),
             )
 
-        def roll(leaving, entering, vector_helps):
-            if leaving is not None:
-                make_room(leaving)
-            for n in range(TILES):
-                if leaving is not None:
-                    if vector_helps and n == TILES - 1:
-                        copy_out(leaving, n, nc.vector.tensor_copy)
-                    else:
-                        copy_out(leaving, n, nc.scalar.copy)
-                if entering is not None:
-                    turn(entering, n)
-
-        def quantise(chunk):
+        def quantise(chunk, part, parts):
+            w = CHUNK_WORDS // parts
             nc.vector.quantize_mx(
-                out=chunk["codes"].bitcast(FP8X4), scales=chunk["scales"], in_=chunk["grouped"][:]
+                out=chunk["operand"][0][:, part * w : (part + 1) * w].bitcast(FP8X4),
+                scales=chunk["operand"][1][:, part * w : (part + 1) * w],
+                in_=chunk["grouped"][:, part * w * PACK : (part + 1) * w * PACK],
             )
 
         def products(total, n, slot_mx, weight_mx, first):
@@ -159,37 +145,72 @@ def tile_gatedmemorymodule_pb_t_kernel(tc, queries, memory_items, wq, U_w, W_w, 
                     stop=(not first and g == PASSES - 1),
                 )
 
-        def blend(h, n, total):
-            cols = slice(h * CHUNK_ROWS, (h + 1) * CHUNK_ROWS)
-            lift = gates.tile([P, CHUNK_ROWS], F32)
-            nc.scalar.activation(out=in_row_order(lift[:]), in_=in_tile_order(total[:]), func=ACT.Tanh, scale=0.5)
+        lifts = {}
+
+        def lift_tile(h, n):
+            lift = gates.tile([P, CHUNK_ROWS], F32, tag="lift")
+            nc.scalar.activation(out=in_row_order(lift[:]), in_=in_tile_order(sums[h][n][:]), func=ACT.Tanh, scale=0.5)
+            lifts[h, n] = lift
+
+        def half_cols(h):
+            return slice(h * CHUNK_ROWS, (h + 1) * CHUNK_ROWS)
+
+        def blend_a(h, n):
             nc.vector.scalar_tensor_tensor(
-                out=lift[:], in0=lift[:], scalar=1.0, in1=step[:, n, cols], op0=ALU.add, op1=ALU.mult
+                out=lifts[h, n][:], in0=lifts[h, n][:], scalar=1.0, in1=step[:, n, half_cols(h)], op0=ALU.add, op1=ALU.mult
             )
+
+        def blend_b(h, n):
             nc.vector.scalar_tensor_tensor(
-                out=new_slots[:, n, cols], in0=lift[:], scalar=0.5, in1=memory_raw[:, n, cols],
+                out=new_slots[:, n, half_cols(h)], in0=lifts[h, n][:], scalar=0.5, in1=memory_raw[:, n, half_cols(h)],
                 op0=ALU.mult, op1=ALU.add,
             )
 
+        def round_slots(h, n, engine_copy):
+            engine_copy(
+                out=rounded[:, n, half_cols(h)].rearrange("p (u q e) -> p u q e", u=2, e=2),
+                in_=new_slots[:, n, half_cols(h)].rearrange("p (q u e) -> p u q e", u=2, e=2),
+            )
+
+        slot_banks = {}
+        slot_grouped = {}
+
+        def turn_slots(h, pair):
+            turned = turn_banks.tile([P, PACK, P], F32, tag="turned")
+            words = rounded[:].bitcast(F32)
+            for i in range(2):
+                for u in range(2):
+                    lo = h * 2 * P + u * P
+                    nc.tensor.transpose(turned[:, 2 * i + u, :], words[:, 2 * pair + i, lo : lo + P], identity[:])
+            slot_banks[h, pair] = turned
+
+        def copy_slots(h, pair, engine_copy):
+            if h not in slot_grouped:
+                grouped = regroup.tile([P, CHUNK_WORDS * PACK], BF16, tag="grouped", align_bytes=64)
+                slot_grouped[h] = grouped
+            target = slot_grouped[h][:, 0 : SLOTS * PACK].bitcast(F32).rearrange("p (n r u) -> p n r u", n=TILES, u=2)
+            engine_copy(
+                out=target[:, 2 * pair : 2 * pair + 2],
+                in_=slot_banks[h, pair][:].rearrange("p (i u) r -> p i r u", u=2),
+            )
+
+        def quantise_slots(h):
+            nc.vector.quantize_mx(
+                out=new_mx[0][:, moving_cols(h)].bitcast(FP8X4),
+                scales=new_mx[1][:, moving_cols(h)],
+                in_=slot_grouped[h][:, 0 : SLOTS * PACK],
+            )
+
         def store_slots(h):
-            cols = slice(h * CHUNK_ROWS, (h + 1) * CHUNK_ROWS)
+            cols = half_cols(h)
             nc.sync.dma_start(
                 out=out_0.rearrange("(p n) k -> p n k", n=TILES)[:, :, cols], in_=new_slots[:, :, cols]
             )
 
-        query_raw = {}
         query = {}
 
-        def query_chunk(c):
-            if c >= QUERY_CHUNKS:
-                return None
-            if c not in query:
-                query[c] = input_chunk(query_raw[c], new_operand(query_mx, "query"), "n g r")
-            return query[c]
-
-        def refill(c):
-            if c + QUERY_BUFFERS < QUERY_CHUNKS:
-                query_raw[c + QUERY_BUFFERS] = load_queries(c + QUERY_BUFFERS)
+        def begin_query(c):
+            query[c] = chunk_of(query_raw[c], new_operand(mx_pool, "chunk"), "n g r")
 
         def begin_answer(c):
             answer = answers.tile([P, TILES, SLOTS], F32)
@@ -200,16 +221,16 @@ def tile_gatedmemorymodule_pb_t_kernel(tc, queries, memory_items, wq, U_w, W_w, 
             query[c]["shift"] = shift
             query[c]["row_sum"] = row_sum
             query[c]["inverse"] = inverse
-            query[c]["sums"] = []
+            query[c]["sums"] = {}
 
         def logit_pass(c, n, g):
             if g == 0:
                 total = sum_banks.tile([P, SLOTS], F32, tag="total")
-                query[c]["sums"].append(total)
+                query[c]["sums"][n] = total
             nc.tensor.matmul_mx(
                 out=query[c]["sums"][n][:],
-                lhsT=query[c]["codes"][:, stationary_cols(n, g)].bitcast(FP8X4),
-                lhsT_scale=query[c]["scales"][:, stationary_cols(n, g)],
+                lhsT=query[c]["operand"][0][:, stationary_cols(n, g)].bitcast(FP8X4),
+                lhsT_scale=query[c]["operand"][1][:, stationary_cols(n, g)],
                 rhs=new_mx[0][:, moving_cols(g)].bitcast(FP8X4),
                 rhs_scale=new_mx[1][:, moving_cols(g)],
                 start=(g == 0),
@@ -241,51 +262,54 @@ def tile_gatedmemorymodule_pb_t_kernel(tc, queries, memory_items, wq, U_w, W_w, 
                 accum_out=query[c]["row_sum"][:, n : n + 1],
             )
 
-        def normalise(c):
-            nc.vector.reciprocal(out=query[c]["inverse"][:], in_=query[c]["row_sum"][:])
-            for n in range(TILES):
-                row = query[c]["answer"][:, n, :]
-                factor = query[c]["inverse"][:, n : n + 1]
-                if c == QUERY_CHUNKS - 1:
-                    nc.vector.tensor_scalar_mul(out=row, in0=row, scalar1=factor)
-                else:
-                    nc.gpsimd.tensor_scalar(
-                        out=row, in0=row, scalar1=factor, scalar2=0.0, op0=ALU.mult, op1=ALU.add
-                    )
-                if (n + 1) % STORE_TILES == 0:
-                    done = slice(n + 1 - STORE_TILES, n + 1)
-                    entries = slice(c * TILES + n + 1 - STORE_TILES, c * TILES + n + 1)
-                    nc.sync.dma_start(out=out_1[:, entries, :], in_=query[c]["answer"][:, done, :])
+        def invert(c, tiles):
+            nc.vector.reciprocal(out=query[c]["inverse"][:, tiles], in_=query[c]["row_sum"][:, tiles])
 
-        memory_raw = load_rows(keep, memory_items, "memory_raw")
-        u_raw = [load_rows(weight_rows, U_w[0:CHUNK_ROWS, :], "weight_raw")]
-        pooled_raw = load_rows(keep, wq, "pooled_raw")
-        w_raw = [load_rows(weight_rows, W_w[0:CHUNK_ROWS, :], "weight_raw")]
-        u_raw.append(load_rows(weight_rows, U_w[CHUNK_ROWS:FEATURES, :], "weight_raw"))
-        w_raw.append(load_rows(weight_rows, W_w[CHUNK_ROWS:FEATURES, :], "weight_raw"))
-        for c in range(QUERY_BUFFERS):
+        def normalise(c, n, on_vector):
+            row = query[c]["answer"][:, n, :]
+            factor = query[c]["inverse"][:, n : n + 1]
+            if on_vector:
+                nc.vector.tensor_scalar_mul(out=row, in0=row, scalar1=factor)
+            else:
+                nc.gpsimd.tensor_scalar(out=row, in0=row, scalar1=factor, scalar2=0.0, op0=ALU.mult, op1=ALU.add)
+
+        def store_answer(c, lo, hi):
+            nc.sync.dma_start(
+                out=out_1[:, c * TILES + lo : c * TILES + hi, :], in_=query[c]["answer"][:, lo:hi, :]
+            )
+
+        S = nc.scalar.copy
+        V = nc.vector.tensor_copy
+        memory_raw = load_rows(keep, memory_items, "memory_raw", 4)
+        pooled_raw = load_rows(keep, wq, "pooled_raw", 2)
+        u_raw = [load_rows(rows_pool, U_w[0:CHUNK_ROWS, :], "rows", 2)]
+        w_raw = [load_rows(rows_pool, W_w[0:CHUNK_ROWS, :], "rows")]
+        u_raw.append(load_rows(rows_pool, U_w[CHUNK_ROWS:FEATURES, :], "rows"))
+        w_raw.append(load_rows(rows_pool, W_w[CHUNK_ROWS:FEATURES, :], "rows"))
+        query_raw = {}
+        for c in range(2):
             query_raw[c] = load_queries(c)
 
         memory_mx = new_operand(keep, "memory")
         pooled_mx = new_operand(keep, "pooled")
-        u_mx = [new_operand(keep, "u%d" % h) for h in range(HALVES)]
-        w_mx = [new_operand(keep, "w%d" % h) for h in range(HALVES)]
+        u_mx = [new_operand(mx_pool, "chunk")]
+        w_mx = [new_operand(mx_pool, "chunk")]
+        u_mx.append(new_operand(mx_pool, "chunk"))
+        w_mx.append(new_operand(mx_pool, "chunk"))
         new_mx = new_operand(keep, "new_slots")
         step = keep.tile([P, TILES, FEATURES], F32)
         new_slots = keep.tile([P, TILES, FEATURES], F32)
+        rounded = keep.tile([P, TILES, FEATURES], BF16)
 
-        memory_chunk = input_chunk(memory_raw, memory_mx, "n g r")
-        pooled_chunk = input_chunk(pooled_raw, pooled_mx, "n g r")
-        u_chunk = [input_chunk(u_raw[h], u_mx[h], "g n r") for h in range(HALVES)]
-        w_chunk = [input_chunk(w_raw[h], w_mx[h], "g n r") for h in range(HALVES)]
-        new_chunk = [slots_chunk(g) for g in range(PASSES)]
+        memory_chunk = chunk_of(memory_raw, memory_mx, "n g r")
+        pooled_chunk = chunk_of(pooled_raw, pooled_mx, "n g r")
+        u_chunk = [chunk_of(u_raw[h], u_mx[h], "g n r") for h in range(HALVES)]
+        w_chunk = [chunk_of(w_raw[h], w_mx[h], "g n r") for h in range(HALVES)]
 
         def difference(n):
             nc.vector.tensor_sub(out=step[:, n, :], in0=pooled_raw[:, n, :], in1=memory_raw[:, n, :])
 
         sums = [{}, {}]
-        first_pair = range(0, TILES // 2)
-        second_pair = range(TILES // 2, TILES)
 
         def start_sums(h, tiles):
             for n in tiles:
@@ -297,72 +321,165 @@ def tile_gatedmemorymodule_pb_t_kernel(tc, queries, memory_items, wq, U_w, W_w, 
             for n in tiles:
                 products(sums[h][n], n, pooled_mx, w_mx[h], False)
 
-        def blend_tiles(h, tiles):
-            for n in tiles:
-                blend(h, n, sums[h][n])
+        LOW = (0, 1)
+        HIGH = (2, 3)
+        ALL = (0, 1, 2, 3)
 
-        roll(None, memory_chunk, False)
-        roll(memory_chunk, u_chunk[0], False)
-        quantise(memory_chunk)
-        roll(u_chunk[0], pooled_chunk, False)
-        quantise(u_chunk[0])
-        start_sums(0, first_pair)
-        roll(pooled_chunk, w_chunk[0], False)
-        quantise(pooled_chunk)
+        def turn_all(chunk, tiles=ALL):
+            for n in tiles:
+                turn(chunk, n)
+
+        def copy_all(chunk, tiles=ALL, eng=S):
+            for n in tiles:
+                copy_out(chunk, n, eng)
+
+
+        turn_all(memory_chunk)
+        copy_all(memory_chunk)
+        quantise(memory_chunk, 0, 1)
+        turn_all(pooled_chunk)
+        copy_all(pooled_chunk)
         difference(0)
         difference(1)
-        start_sums(0, second_pair)
-        roll(w_chunk[0], u_chunk[1], False)
-        quantise(w_chunk[0])
+        quantise(pooled_chunk, 0, 1)
+        turn_all(u_chunk[0])
+        copy_all(u_chunk[0])
         difference(2)
+        quantise(u_chunk[0], 0, 1)
+        turn_all(w_chunk[0])
+        copy_all(w_chunk[0])
+        start_sums(0, ALL)
         difference(3)
-        finish_sums(0, first_pair)
-        roll(u_chunk[1], w_chunk[1], False)
-        quantise(u_chunk[1])
-        blend_tiles(0, first_pair)
-        finish_sums(0, second_pair)
-        roll(w_chunk[1], query_chunk(0), False)
-        refill(0)
-        quantise(w_chunk[1])
-        start_sums(1, first_pair)
-        blend_tiles(0, second_pair)
+        for n in ALL:
+            sort_words(u_chunk[1], n, S)
+        quantise(w_chunk[0], 0, 1)
+        for n in ALL:
+            sort_words(w_chunk[1], n, V)
+        turn_all(u_chunk[1])
+        copy_out(u_chunk[1], 0, S)
+        copy_out(u_chunk[1], 1, V)
+        copy_out(u_chunk[1], 2, S)
+        copy_out(u_chunk[1], 3, V)
+        finish_sums(0, ALL)
+        quantise(u_chunk[1], 0, 1)
+        turn_all(w_chunk[1])
+        for n in ALL:
+            lift_tile(0, n)
+        blend_a(0, 0)
+        blend_a(0, 1)
+        blend_b(0, 0)
+        blend_b(0, 1)
+        copy_out(w_chunk[1], 0, S)
+        copy_out(w_chunk[1], 1, S)
+        copy_out(w_chunk[1], 2, V)
+        copy_out(w_chunk[1], 3, S)
+        begin_query(0)
+        turn_all(query[0], LOW)
+        quantise(w_chunk[1], 0, 2)
+        quantise(w_chunk[1], 1, 2)
+        round_slots(0, 0, S)
+        round_slots(0, 1, S)
+        for n in ALL:
+            start_sums(1, (n,))
+            finish_sums(1, (n,))
+        blend_a(0, 2)
+        blend_a(0, 3)
+        blend_b(0, 2)
+        blend_b(0, 3)
+        copy_all(query[0], LOW)
+        query_raw[2] = load_queries(2)
+        lift_tile(1, 0)
+        lift_tile(1, 1)
+        round_slots(0, 2, S)
+        lift_tile(1, 2)
+        round_slots(0, 3, S)
         store_slots(0)
-        roll(query_chunk(0), None, False)
-        finish_sums(1, first_pair)
-        start_sums(1, second_pair)
-        finish_sums(1, second_pair)
-        blend_tiles(1, first_pair)
-        roll(None, new_chunk[0], False)
-        blend_tiles(1, second_pair)
-        store_slots(1)
-        quantise(query_chunk(0))
-        roll(new_chunk[0], new_chunk[1], False)
-        quantise(new_chunk[0])
+        turn_slots(0, 0)
+        turn_slots(0, 1)
+        lift_tile(1, 3)
+        turn_all(query[0], HIGH)
+        query_raw[3] = load_queries(3)
+        blend_a(1, 0)
+        blend_a(1, 1)
+        blend_b(1, 0)
+        blend_a(1, 2)
+        blend_b(1, 1)
+        copy_slots(0, 0, S)
+        round_slots(1, 0, S)
+        copy_slots(0, 1, S)
+        round_slots(1, 1, S)
+        blend_a(1, 3)
+        blend_b(1, 2)
+        quantise(query[0], 0, 2)
+        blend_b(1, 3)
+        round_slots(1, 2, V)
+        quantise_slots(0)
+        round_slots(1, 3, V)
+        copy_all(query[0], HIGH)
+        begin_query(1)
+        turn_all(query[1], LOW)
+        turn_slots(1, 0)
+        turn_slots(1, 1)
+        quantise(query[0], 1, 2)
+        copy_slots(1, 0, S)
+        copy_slots(1, 1, S)
+        quantise_slots(1)
         begin_answer(0)
-        for n in range(TILES):
+        for n in ALL:
             logit_pass(0, n, 0)
-        roll(new_chunk[1], query_chunk(1), False)
-        refill(1)
-        quantise(new_chunk[1])
-        for n in range(TILES):
+        copy_all(query[1], LOW)
+        turn_all(query[1], HIGH)
+        copy_all(query[1], HIGH)
+        store_slots(1)
+        for n in ALL:
             logit_pass(0, n, 1)
+        query_raw[4] = load_queries(4)
+        query_raw[5] = load_queries(5)
+        quantise(query[1], 0, 2)
+        quantise(query[1], 1, 2)
 
-        roll(query_chunk(1), query_chunk(2), False)
-        refill(2)
-        quantise(query_chunk(1))
-        roll(query_chunk(2), query_chunk(3), False)
-        refill(3)
-        for c in range(QUERY_CHUNKS):
-            if c + 1 < QUERY_CHUNKS:
-                begin_answer(c + 1)
-            for n in range(TILES):
-                leave_bank(c, n)
-                if c + 1 < QUERY_CHUNKS:
-                    multiply(c + 1, n)
-                exponential(c, n)
-            if c + 3 < QUERY_CHUNKS:
-                roll(query_chunk(c + 3), query_chunk(c + 4), True)
-                refill(c + 4)
+        def finish(c, pair):
+            invert(c, slice(pair[0], pair[0] + 2))
+            for n in pair:
+                normalise(c, n, c == QUERY_CHUNKS - 1)
+
+        def store(c, pair):
+            store_answer(c, pair[0], pair[0] + 2)
+
+        QS = {LOW: (), HIGH: ()}
+
+        def sort_step(i):
+            if i < len(steps) and steps[i][0] + 2 < QUERY_CHUNKS:
+                c, pair = steps[i]
+                if pair == LOW:
+                    begin_query(c + 2)
+                for n in QS[pair]:
+                    sort_words(query[c + 2], n, V)
+
+        steps = [(c, pair) for c in range(QUERY_CHUNKS) for pair in (LOW, HIGH)]
+        sort_step(0)
+        for i, (c, pair) in enumerate(steps):
+            if pair == LOW and c > 0:
+                begin_answer(c)
             if c + 2 < QUERY_CHUNKS:
-                quantise(query_chunk(c + 2))
-            normalise(c)
+                turn_all(query[c + 2], pair)
+                copy_all(query[c + 2], pair)
+            if c > 0:
+                for n in pair:
+                    multiply(c, n)
+            if i > 1:
+                finish(*steps[i - 2])
+            for n in pair:
+                leave_bank(c, n)
+            for n in pair:
+                exponential(c, n)
+            sort_step(i + 1)
+            if c + 2 < QUERY_CHUNKS:
+                quantise(query[c + 2], pair[0] // 2, 2)
+            if i > 1:
+                store(*steps[i - 2])
+            if pair == HIGH and c + 6 < QUERY_CHUNKS:
+                query_raw[c + 6] = load_queries(c + 6)
+        for step_i in range(len(steps) - 2, len(steps)):
+            finish(*steps[step_i])
+            store(*steps[step_i])

@@ -438,48 +438,73 @@ def tile_gatedmemorymodule_pb_t_kernel(tc, queries, memory_items, wq, U_w, W_w, 
         quantise(query[1], 0, 2)
         quantise(query[1], 1, 2)
 
-        def finish(c, pair):
-            invert(c, slice(pair[0], pair[0] + 2))
-            for n in pair:
-                normalise(c, n, c == QUERY_CHUNKS - 1)
-
-        def store(c, pair):
-            store_answer(c, pair[0], pair[0] + 2)
-
-        QS = {LOW: (), HIGH: ()}
-
-        def sort_step(i):
-            if i < len(steps) and steps[i][0] + 2 < QUERY_CHUNKS:
-                c, pair = steps[i]
-                if pair == LOW:
-                    begin_query(c + 2)
-                for n in QS[pair]:
-                    sort_words(query[c + 2], n, V)
+        def finish(c, tiles, vec):
+            invert(c, slice(tiles[0], tiles[0] + len(tiles)))
+            for n in tiles:
+                normalise(c, n, vec or n in NV)
+            store_answer(c, tiles[0], tiles[0] + len(tiles))
 
         steps = [(c, pair) for c in range(QUERY_CHUNKS) for pair in (LOW, HIGH)]
-        sort_step(0)
-        for i, (c, pair) in enumerate(steps):
-            if pair == LOW and c > 0:
-                begin_answer(c)
-            if c + 2 < QUERY_CHUNKS:
-                turn_all(query[c + 2], pair)
-                copy_all(query[c + 2], pair)
-            if c > 0:
+        NS = len(steps)
+        VC = ()
+        NV = ()
+        SORTS = {0: (), 1: ()}
+
+        def do_S(j):
+            if 4 <= j < NS:
+                c, pair = steps[j]
+                if pair == LOW:
+                    begin_query(c)
+                for k in SORTS[j % 2]:
+                    sort_words(query[c], pair[k], V)
+
+        def do_T(j):
+            if 4 <= j < NS:
+                c, pair = steps[j]
+                turn_all(query[c], pair)
+                if pair == HIGH and c + 4 < QUERY_CHUNKS:
+                    query_raw[c + 4] = load_queries(c + 4)
+
+        def do_C(j):
+            if 4 <= j < NS:
+                for k, n in enumerate(steps[j][1]):
+                    copy_out(query[steps[j][0]], n, V if (j % 2, k) in VC else S)
+
+        def do_Q(j):
+            if 4 <= j < NS:
+                quantise(query[steps[j][0]], steps[j][1][0] // 2, 2)
+
+        def do_M(j):
+            if 2 <= j < NS:
+                c, pair = steps[j]
+                if pair == LOW:
+                    begin_answer(c)
                 for n in pair:
                     multiply(c, n)
-            if i > 1:
-                finish(*steps[i - 2])
-            for n in pair:
-                leave_bank(c, n)
-            for n in pair:
-                exponential(c, n)
-            sort_step(i + 1)
-            if c + 2 < QUERY_CHUNKS:
-                quantise(query[c + 2], pair[0] // 2, 2)
-            if i > 1:
-                store(*steps[i - 2])
-            if pair == HIGH and c + 6 < QUERY_CHUNKS:
-                query_raw[c + 6] = load_queries(c + 6)
-        for step_i in range(len(steps) - 2, len(steps)):
-            finish(*steps[step_i])
-            store(*steps[step_i])
+
+        def do_L(j):
+            if 0 <= j < NS:
+                for n in steps[j][1]:
+                    leave_bank(steps[j][0], n)
+
+        def do_E(j):
+            if 0 <= j < NS:
+                for n in steps[j][1]:
+                    exponential(steps[j][0], n)
+
+        def do_F(j):
+            if 0 <= j < NS - 1:
+                finish(steps[j][0], steps[j][1], j >= NS - 2)
+            elif j == NS - 1:
+                for n in steps[j][1]:
+                    finish(steps[j][0], (n,), True)
+
+        for i in range(-2, NS + 4):
+            do_S(i + 5)
+            do_T(i + 3)
+            do_C(i + 3)
+            do_M(i + 0)
+            do_F(i + -2)
+            do_Q(i + 2)
+            do_L(i + 0)
+            do_E(i + -1)

@@ -77,7 +77,10 @@ def tile_gatedmemorymodule_pb_t_kernel(tc, queries, memory_items, wq, U_w, W_w, 
 
         def load_queries(c):
             raw = rows_pool.tile([P, TILES, FEATURES], BF16, name="rows")
-            nc.sync.dma_start(out=raw[:], in_=queries[:, c * TILES : (c + 1) * TILES, :])
+            for i in range(2):
+                part = slice(i * TILES // 2, (i + 1) * TILES // 2)
+                first = c * TILES
+                nc.sync.dma_start(out=raw[:, part, :], in_=queries[:, first + part.start : first + part.stop, :])
             return raw
 
         def new_operand(pool, label):
@@ -281,11 +284,11 @@ def tile_gatedmemorymodule_pb_t_kernel(tc, queries, memory_items, wq, U_w, W_w, 
         S = nc.scalar.copy
         V = nc.vector.tensor_copy
         memory_raw = load_rows(keep, memory_items, "memory_raw", 4)
-        pooled_raw = load_rows(keep, wq, "pooled_raw", 2)
+        pooled_raw = load_rows(keep, wq, "pooled_raw", 4)
         u_raw = [load_rows(rows_pool, U_w[0:CHUNK_ROWS, :], "rows", 2)]
-        w_raw = [load_rows(rows_pool, W_w[0:CHUNK_ROWS, :], "rows")]
-        u_raw.append(load_rows(rows_pool, U_w[CHUNK_ROWS:FEATURES, :], "rows"))
-        w_raw.append(load_rows(rows_pool, W_w[CHUNK_ROWS:FEATURES, :], "rows"))
+        w_raw = [load_rows(rows_pool, W_w[0:CHUNK_ROWS, :], "rows", 2)]
+        u_raw.append(load_rows(rows_pool, U_w[CHUNK_ROWS:FEATURES, :], "rows", 2))
+        w_raw.append(load_rows(rows_pool, W_w[CHUNK_ROWS:FEATURES, :], "rows", 2))
         query_raw = {}
         for c in range(2):
             query_raw[c] = load_queries(c)
@@ -334,6 +337,7 @@ def tile_gatedmemorymodule_pb_t_kernel(tc, queries, memory_items, wq, U_w, W_w, 
                 copy_out(chunk, n, eng)
 
 
+        begin_query(0)
         turn_all(memory_chunk)
         copy_all(memory_chunk)
         quantise(memory_chunk, 0, 1)
@@ -348,130 +352,97 @@ def tile_gatedmemorymodule_pb_t_kernel(tc, queries, memory_items, wq, U_w, W_w, 
         quantise(u_chunk[0], 0, 1)
         turn_all(w_chunk[0])
         copy_all(w_chunk[0])
-        start_sums(0, ALL)
         difference(3)
-        for n in ALL:
-            sort_words(u_chunk[1], n, S)
         quantise(w_chunk[0], 0, 1)
-        for n in ALL:
-            sort_words(w_chunk[1], n, V)
         turn_all(u_chunk[1])
-        copy_out(u_chunk[1], 0, S)
-        copy_out(u_chunk[1], 1, V)
-        copy_out(u_chunk[1], 2, S)
-        copy_out(u_chunk[1], 3, V)
-        finish_sums(0, ALL)
+        copy_all(u_chunk[1])
         quantise(u_chunk[1], 0, 1)
         turn_all(w_chunk[1])
-        for n in ALL:
-            lift_tile(0, n)
-        blend_a(0, 0)
-        blend_a(0, 1)
-        blend_b(0, 0)
-        blend_b(0, 1)
-        copy_out(w_chunk[1], 0, S)
-        copy_out(w_chunk[1], 1, S)
-        copy_out(w_chunk[1], 2, V)
-        copy_out(w_chunk[1], 3, S)
-        begin_query(0)
-        turn_all(query[0], LOW)
-        quantise(w_chunk[1], 0, 2)
-        quantise(w_chunk[1], 1, 2)
-        round_slots(0, 0, S)
-        round_slots(0, 1, S)
-        for n in ALL:
-            start_sums(1, (n,))
-            finish_sums(1, (n,))
-        blend_a(0, 2)
-        blend_a(0, 3)
-        blend_b(0, 2)
-        blend_b(0, 3)
+        copy_all(w_chunk[1])
+        turn_all(query[0])
         copy_all(query[0], LOW)
+        copy_out(query[0], 2, S)
+        copy_out(query[0], 3, V)
+        quantise(w_chunk[1], 0, 1)
         query_raw[2] = load_queries(2)
-        lift_tile(1, 0)
-        lift_tile(1, 1)
-        round_slots(0, 2, S)
-        lift_tile(1, 2)
-        round_slots(0, 3, S)
-        store_slots(0)
+        query_raw[3] = load_queries(3)
+        begin_query(1)
+        tiles = [(h, n) for h in range(HALVES) for n in range(TILES)]
+        for i in range(len(tiles) + 1):
+            if i < len(tiles):
+                h, n = tiles[i]
+                start_sums(h, (n,))
+                finish_sums(h, (n,))
+                lift_tile(h, n)
+                blend_a(h, n)
+            if 0 < i:
+                blend_b(*tiles[i - 1])
+            if 3 <= i < len(tiles):
+                round_slots(*tiles[i - 3], S)
         turn_slots(0, 0)
         turn_slots(0, 1)
-        lift_tile(1, 3)
-        turn_all(query[0], HIGH)
-        query_raw[3] = load_queries(3)
-        blend_a(1, 0)
-        blend_a(1, 1)
-        blend_b(1, 0)
-        blend_a(1, 2)
-        blend_b(1, 1)
-        copy_slots(0, 0, S)
-        round_slots(1, 0, S)
-        copy_slots(0, 1, S)
-        round_slots(1, 1, S)
-        blend_a(1, 3)
-        blend_b(1, 2)
-        quantise(query[0], 0, 2)
-        blend_b(1, 3)
-        round_slots(1, 2, V)
-        quantise_slots(0)
-        round_slots(1, 3, V)
-        copy_all(query[0], HIGH)
-        begin_query(1)
         turn_all(query[1], LOW)
+        store_slots(0)
+        for i in range(len(tiles) - 3, len(tiles) - 2):
+            round_slots(*tiles[i], S)
+        copy_slots(0, 0, S)
+        copy_slots(0, 1, S)
         turn_slots(1, 0)
-        turn_slots(1, 1)
+        for i in range(len(tiles) - 2, len(tiles)):
+            round_slots(*tiles[i], V)
+        quantise_slots(0)
+        quantise(query[0], 0, 2)
         quantise(query[0], 1, 2)
-        copy_slots(1, 0, S)
-        copy_slots(1, 1, S)
-        quantise_slots(1)
+        turn_slots(1, 1)
         begin_answer(0)
         for n in ALL:
             logit_pass(0, n, 0)
-        copy_all(query[1], LOW)
-        turn_all(query[1], HIGH)
-        copy_all(query[1], HIGH)
+        copy_slots(1, 0, S)
+        copy_slots(1, 1, S)
+        quantise_slots(1)
         store_slots(1)
-        for n in ALL:
-            logit_pass(0, n, 1)
         query_raw[4] = load_queries(4)
         query_raw[5] = load_queries(5)
+        for n in ALL:
+            logit_pass(0, n, 1)
+        copy_all(query[1], LOW)
         quantise(query[1], 0, 2)
-        quantise(query[1], 1, 2)
 
         def finish(c, tiles, vec):
             invert(c, slice(tiles[0], tiles[0] + len(tiles)))
             for n in tiles:
-                normalise(c, n, vec or n in NV)
+                normalise(c, n, vec or (c, n) in NVEC)
             store_answer(c, tiles[0], tiles[0] + len(tiles))
 
         steps = [(c, pair) for c in range(QUERY_CHUNKS) for pair in (LOW, HIGH)]
         NS = len(steps)
-        VC = ()
-        NV = ()
-        SORTS = {0: (), 1: ()}
-
-        def do_S(j):
-            if 4 <= j < NS:
-                c, pair = steps[j]
-                if pair == LOW:
-                    begin_query(c)
-                for k in SORTS[j % 2]:
-                    sort_words(query[c], pair[k], V)
+        NVEC = ()
+        VCOPY = ()
+        P0 = 3
 
         def do_T(j):
-            if 4 <= j < NS:
+            if P0 <= j < NS:
                 c, pair = steps[j]
+                if pair == LOW and c > 1:
+                    begin_query(c)
                 turn_all(query[c], pair)
-                if pair == HIGH and c + 4 < QUERY_CHUNKS:
-                    query_raw[c + 4] = load_queries(c + 4)
+                if pair == HIGH and 6 <= c + 5 < QUERY_CHUNKS:
+                    query_raw[c + 5] = load_queries(c + 5)
 
         def do_C(j):
-            if 4 <= j < NS:
+            if P0 <= j < NS:
                 for k, n in enumerate(steps[j][1]):
-                    copy_out(query[steps[j][0]], n, V if (j % 2, k) in VC else S)
+                    if (j, k) not in VCOPY:
+                        copy_out(query[steps[j][0]], n, S)
+
+        def do_D(j):
+            if P0 <= j < NS:
+                for k, n in enumerate(steps[j][1]):
+                    if (j, k) in VCOPY:
+                        copy_out(query[steps[j][0]], n, V)
 
         def do_Q(j):
-            if 4 <= j < NS:
+            if P0 <= j < NS:
                 quantise(query[steps[j][0]], steps[j][1][0] // 2, 2)
 
         def do_M(j):
@@ -499,12 +470,12 @@ def tile_gatedmemorymodule_pb_t_kernel(tc, queries, memory_items, wq, U_w, W_w, 
                 for n in steps[j][1]:
                     finish(steps[j][0], (n,), True)
 
-        for i in range(-2, NS + 4):
-            do_S(i + 5)
+        for i in range(-3, NS + 4):
             do_T(i + 3)
             do_C(i + 3)
             do_M(i + 0)
             do_F(i + -2)
             do_Q(i + 2)
             do_L(i + 0)
+            do_D(i + 3)
             do_E(i + -1)

@@ -67,6 +67,14 @@ def tile_gatedmemorymodule_pb_t_kernel(tc, queries, memory_items, wq, U_w, W_w, 
         identity = keep.tile([P, P], F32)
         make_identity(nc, identity[:])
 
+        still = keep.tile([P, CHUNK_ROWS], BF16, name="still")
+        nc.vector.memset(still[:], 0.0)
+
+        def stir(times):
+            for i in range(times):
+                unread = sum_banks.tile([P, CHUNK_ROWS], F32, tag="total")
+                nc.tensor.matmul(out=unread[:], lhsT=still[:, 0:P], rhs=still[:], start=True, stop=True)
+
         def load_rows(pool, rows, label, pieces=1):
             raw = pool.tile([P, TILES, FEATURES], BF16, name=label)
             view = rows.rearrange("(p n) k -> p n k", n=TILES)
@@ -338,27 +346,34 @@ def tile_gatedmemorymodule_pb_t_kernel(tc, queries, memory_items, wq, U_w, W_w, 
 
 
         begin_query(0)
+        stir(6)
         turn_all(memory_chunk)
         copy_all(memory_chunk)
         quantise(memory_chunk, 0, 1)
+        stir(1)
         turn_all(pooled_chunk)
         copy_all(pooled_chunk)
         difference(0)
         difference(1)
         quantise(pooled_chunk, 0, 1)
+        stir(1)
         turn_all(u_chunk[0])
         copy_all(u_chunk[0])
         difference(2)
         quantise(u_chunk[0], 0, 1)
+        stir(1)
         turn_all(w_chunk[0])
         copy_all(w_chunk[0])
         difference(3)
         quantise(w_chunk[0], 0, 1)
+        stir(1)
         turn_all(u_chunk[1])
         copy_all(u_chunk[1])
         quantise(u_chunk[1], 0, 1)
+        stir(1)
         turn_all(w_chunk[1])
         copy_all(w_chunk[1])
+        stir(1)
         turn_all(query[0])
         copy_all(query[0], LOW)
         copy_out(query[0], 2, S)

@@ -346,7 +346,7 @@ def tile_gatedmemorymodule_pb_t_kernel(tc, queries, memory_items, wq, U_w, W_w, 
 
 
         begin_query(0)
-        stir(6)
+        stir(4)
         turn_all(memory_chunk)
         copy_all(memory_chunk)
         quantise(memory_chunk, 0, 1)
@@ -358,29 +358,32 @@ def tile_gatedmemorymodule_pb_t_kernel(tc, queries, memory_items, wq, U_w, W_w, 
         quantise(pooled_chunk, 0, 1)
         stir(1)
         turn_all(u_chunk[0])
+        query_raw[2] = load_queries(2)
         copy_all(u_chunk[0])
         difference(2)
         quantise(u_chunk[0], 0, 1)
         stir(1)
         turn_all(w_chunk[0])
+        query_raw[3] = load_queries(3)
         copy_all(w_chunk[0])
         difference(3)
         quantise(w_chunk[0], 0, 1)
         stir(1)
         turn_all(u_chunk[1])
+        query_raw[4] = load_queries(4)
         copy_all(u_chunk[1])
         quantise(u_chunk[1], 0, 1)
         stir(1)
         turn_all(w_chunk[1])
+        query_raw[5] = load_queries(5)
         copy_all(w_chunk[1])
+        quantise(w_chunk[1], 0, 1)
         stir(1)
         turn_all(query[0])
         copy_all(query[0], LOW)
-        copy_out(query[0], 2, S)
-        copy_out(query[0], 3, V)
-        quantise(w_chunk[1], 0, 1)
-        query_raw[2] = load_queries(2)
-        query_raw[3] = load_queries(3)
+        copy_out(query[0], 2, V)
+        copy_out(query[0], 3, S)
+        quantise(query[0], 0, 1)
         begin_query(1)
         tiles = [(h, n) for h in range(HALVES) for n in range(TILES)]
         for i in range(len(tiles) + 1):
@@ -402,38 +405,44 @@ def tile_gatedmemorymodule_pb_t_kernel(tc, queries, memory_items, wq, U_w, W_w, 
             round_slots(*tiles[i], S)
         copy_slots(0, 0, S)
         copy_slots(0, 1, S)
-        turn_slots(1, 0)
+        copy_all(query[1], LOW)
+        stir(2)
+        turn_all(query[1], HIGH)
+        query_raw[6] = load_queries(6)
         for i in range(len(tiles) - 2, len(tiles)):
             round_slots(*tiles[i], V)
         quantise_slots(0)
-        quantise(query[0], 0, 2)
-        quantise(query[0], 1, 2)
+        turn_slots(1, 0)
         turn_slots(1, 1)
         begin_answer(0)
         for n in ALL:
             logit_pass(0, n, 0)
         copy_slots(1, 0, S)
         copy_slots(1, 1, S)
+        quantise(query[1], 0, 2)
         quantise_slots(1)
         store_slots(1)
-        query_raw[4] = load_queries(4)
-        query_raw[5] = load_queries(5)
         for n in ALL:
             logit_pass(0, n, 1)
-        copy_all(query[1], LOW)
-        quantise(query[1], 0, 2)
+        copy_all(query[1], HIGH)
+        quantise(query[1], 1, 2)
 
-        def finish(c, tiles, vec):
+        def finish(c, tiles, vec, sharing):
             invert(c, slice(tiles[0], tiles[0] + len(tiles)))
-            for n in tiles:
-                normalise(c, n, vec or (c, n) in NVEC)
-            store_answer(c, tiles[0], tiles[0] + len(tiles))
+            for k, n in enumerate(tiles):
+                if not (sharing and k == 1):
+                    normalise(c, n, vec)
+            if not sharing:
+                store_answer(c, tiles[0], tiles[0] + len(tiles))
+
+        def shares(j):
+            return j < 14
 
         steps = [(c, pair) for c in range(QUERY_CHUNKS) for pair in (LOW, HIGH)]
         NS = len(steps)
         NVEC = ()
         VCOPY = ()
-        P0 = 3
+        P0 = 4
 
         def do_T(j):
             if P0 <= j < NS:
@@ -480,10 +489,16 @@ def tile_gatedmemorymodule_pb_t_kernel(tc, queries, memory_items, wq, U_w, W_w, 
 
         def do_F(j):
             if 0 <= j < NS - 1:
-                finish(steps[j][0], steps[j][1], j >= NS - 2)
+                finish(steps[j][0], steps[j][1], j >= NS - 2, shares(j))
             elif j == NS - 1:
                 for n in steps[j][1]:
-                    finish(steps[j][0], (n,), True)
+                    finish(steps[j][0], (n,), True, False)
+
+        def do_G(j):
+            if 0 <= j < NS and shares(j):
+                c, tiles = steps[j]
+                normalise(c, tiles[1], True)
+                store_answer(c, tiles[0], tiles[0] + len(tiles))
 
         for i in range(-3, NS + 4):
             do_T(i + 3)
@@ -492,5 +507,6 @@ def tile_gatedmemorymodule_pb_t_kernel(tc, queries, memory_items, wq, U_w, W_w, 
             do_F(i + -2)
             do_Q(i + 2)
             do_L(i + 0)
+            do_G(i + -2)
             do_D(i + 3)
             do_E(i + -1)

@@ -379,7 +379,9 @@ def tile_gatedmemorymodule_pb_t_kernel(tc, queries, memory_items, wq, U_w, W_w, 
         copy_all(w_chunk[1])
         quantise(w_chunk[1], 0, 1)
         stir(1)
-        turn_all(query[0])
+        turn_all(query[0], LOW)
+        stir(1)
+        turn_all(query[0], HIGH)
         copy_all(query[0], LOW)
         copy_out(query[0], 2, V)
         copy_out(query[0], 3, S)
@@ -406,21 +408,24 @@ def tile_gatedmemorymodule_pb_t_kernel(tc, queries, memory_items, wq, U_w, W_w, 
         copy_slots(0, 0, S)
         copy_slots(0, 1, S)
         copy_all(query[1], LOW)
-        stir(2)
-        turn_all(query[1], HIGH)
-        query_raw[6] = load_queries(6)
         for i in range(len(tiles) - 2, len(tiles)):
             round_slots(*tiles[i], V)
         quantise_slots(0)
+        stir(2)
         turn_slots(1, 0)
         turn_slots(1, 1)
+        turn_all(query[1], HIGH)
+        query_raw[6] = load_queries(6)
         begin_answer(0)
         for n in ALL:
             logit_pass(0, n, 0)
         copy_slots(1, 0, S)
         copy_slots(1, 1, S)
-        quantise(query[1], 0, 2)
+        begin_query(2)
+        for n in (0, 1, 2, 3):
+            sort_words(query[2], n, V)
         quantise_slots(1)
+        quantise(query[1], 0, 2)
         store_slots(1)
         for n in ALL:
             logit_pass(0, n, 1)
@@ -447,7 +452,7 @@ def tile_gatedmemorymodule_pb_t_kernel(tc, queries, memory_items, wq, U_w, W_w, 
         def do_T(j):
             if P0 <= j < NS:
                 c, pair = steps[j]
-                if pair == LOW and c > 1:
+                if pair == LOW and c > 2:
                     begin_query(c)
                 turn_all(query[c], pair)
                 if pair == HIGH and 6 <= c + 5 < QUERY_CHUNKS:

@@ -85,10 +85,7 @@ def tile_gatedmemorymodule_pb_t_kernel(tc, queries, memory_items, wq, U_w, W_w, 
 
         def load_queries(c):
             raw = rows_pool.tile([P, TILES, FEATURES], BF16, name="rows")
-            for i in range(2):
-                part = slice(i * TILES // 2, (i + 1) * TILES // 2)
-                first = c * TILES
-                nc.sync.dma_start(out=raw[:, part, :], in_=queries[:, first + part.start : first + part.stop, :])
+            nc.sync.dma_start(out=raw[:], in_=queries[:, c * TILES : (c + 1) * TILES, :])
             return raw
 
         def new_operand(pool, label):
@@ -291,10 +288,10 @@ def tile_gatedmemorymodule_pb_t_kernel(tc, queries, memory_items, wq, U_w, W_w, 
 
         S = nc.scalar.copy
         V = nc.vector.tensor_copy
-        memory_raw = load_rows(keep, memory_items, "memory_raw", 4)
-        pooled_raw = load_rows(keep, wq, "pooled_raw", 4)
-        u_raw = [load_rows(rows_pool, U_w[0:CHUNK_ROWS, :], "rows", 2)]
-        w_raw = [load_rows(rows_pool, W_w[0:CHUNK_ROWS, :], "rows", 2)]
+        memory_raw = load_rows(keep, memory_items, "memory_raw", 2)
+        pooled_raw = load_rows(keep, wq, "pooled_raw", 1)
+        u_raw = [load_rows(rows_pool, U_w[0:CHUNK_ROWS, :], "rows", 1)]
+        w_raw = [load_rows(rows_pool, W_w[0:CHUNK_ROWS, :], "rows", 1)]
         u_raw.append(load_rows(rows_pool, U_w[CHUNK_ROWS:FEATURES, :], "rows", 2))
         w_raw.append(load_rows(rows_pool, W_w[CHUNK_ROWS:FEATURES, :], "rows", 2))
         query_raw = {}

@@ -115,8 +115,11 @@ def tile_gatedmemorymodule_pb_t_kernel(tc, queries, memory_items, wq, U_w, W_w, 
             )
             chunk["blocks"][n] = [words[:, j * P : (j + 1) * P] for j in range(PACK)]
 
-        def turn(chunk, n):
-            turned = turn_banks.tile([P, PACK, P], F32, tag="turned")
+        def turn(chunk, n, spare=False):
+            if spare:
+                turned = sum_banks.tile([P, PACK, P], F32, tag="total")
+            else:
+                turned = turn_banks.tile([P, PACK, P], F32, tag="turned")
             for j in range(PACK):
                 nc.tensor.transpose(turned[:, j, :], chunk["blocks"][n][j], identity[:])
             chunk["banks"][n] = turned
@@ -333,9 +336,9 @@ def tile_gatedmemorymodule_pb_t_kernel(tc, queries, memory_items, wq, U_w, W_w, 
         HIGH = (2, 3)
         ALL = (0, 1, 2, 3)
 
-        def turn_all(chunk, tiles=ALL):
+        def turn_all(chunk, tiles=ALL, spare=False):
             for n in tiles:
-                turn(chunk, n)
+                turn(chunk, n, spare)
 
         def copy_all(chunk, tiles=ALL, eng=S):
             for n in tiles:
@@ -375,19 +378,14 @@ def tile_gatedmemorymodule_pb_t_kernel(tc, queries, memory_items, wq, U_w, W_w, 
         query_raw[5] = load_queries(5)
         copy_all(w_chunk[1])
         quantise(w_chunk[1], 0, 1)
-        stir(1)
-        turn_all(query[0], LOW)
-        stir(1)
-        turn_all(query[0], HIGH)
-        copy_all(query[0], LOW)
-        copy_out(query[0], 2, V)
-        copy_out(query[0], 3, S)
-        quantise(query[0], 0, 1)
         begin_query(1)
         tiles = [(h, n) for h in range(HALVES) for n in range(TILES)]
         for i in range(len(tiles) + 1):
             if i < len(tiles):
                 h, n = tiles[i]
+                if i == 99:
+                    turn_slots(0, 0)
+                    turn_slots(0, 1)
                 start_sums(h, (n,))
                 finish_sums(h, (n,))
                 lift_tile(h, n)
@@ -398,37 +396,35 @@ def tile_gatedmemorymodule_pb_t_kernel(tc, queries, memory_items, wq, U_w, W_w, 
                 round_slots(*tiles[i - 3], S)
         turn_slots(0, 0)
         turn_slots(0, 1)
-        turn_all(query[1], LOW)
+        turn_all(query[0], ALL, True)
         store_slots(0)
         for i in range(len(tiles) - 3, len(tiles) - 2):
             round_slots(*tiles[i], S)
         copy_slots(0, 0, S)
         copy_slots(0, 1, S)
-        copy_all(query[1], LOW)
+        copy_all(query[0], LOW)
         for i in range(len(tiles) - 2, len(tiles)):
             round_slots(*tiles[i], V)
         quantise_slots(0)
-        stir(2)
         turn_slots(1, 0)
         turn_slots(1, 1)
-        turn_all(query[1], HIGH)
-        query_raw[6] = load_queries(6)
-        begin_answer(0)
-        for n in ALL:
-            logit_pass(0, n, 0)
+        turn_all(query[1], LOW)
+        quantise(query[0], 0, 2)
         copy_slots(1, 0, S)
         copy_slots(1, 1, S)
-        begin_query(2)
-        for n in (0, 1, 2, 3):
-            sort_words(query[2], n, V)
+        copy_all(query[0], HIGH, S)
         quantise_slots(1)
-        quantise(query[1], 0, 2)
+        quantise(query[0], 1, 2)
         store_slots(1)
-        for n in ALL:
-            logit_pass(0, n, 1)
-        copy_all(query[1], HIGH)
-        quantise(query[1], 1, 2)
-
+        begin_answer(0)
+        for n in LOW:
+            multiply(0, n)
+        for n in HIGH:
+            multiply(0, n)
+        copy_all(query[1], LOW)
+        for n in (2, 3):
+            sort_words(query[1], n, V)
+        quantise(query[1], 0, 2)
         def finish(c, tiles, vec, sharing):
             invert(c, slice(tiles[0], tiles[0] + len(tiles)))
             for k, n in enumerate(tiles):
@@ -444,12 +440,12 @@ def tile_gatedmemorymodule_pb_t_kernel(tc, queries, memory_items, wq, U_w, W_w, 
         NS = len(steps)
         NVEC = ()
         VCOPY = ()
-        P0 = 4
+        P0 = 3
 
         def do_T(j):
             if P0 <= j < NS:
                 c, pair = steps[j]
-                if pair == LOW and c > 2:
+                if pair == LOW and c > 1:
                     begin_query(c)
                 turn_all(query[c], pair)
                 if pair == HIGH and 6 <= c + 5 < QUERY_CHUNKS:
@@ -503,12 +499,12 @@ def tile_gatedmemorymodule_pb_t_kernel(tc, queries, memory_items, wq, U_w, W_w, 
                 store_answer(c, tiles[0], tiles[0] + len(tiles))
 
         for i in range(-3, NS + 4):
-            do_T(i + 3)
-            do_C(i + 3)
+            do_T(i + 2)
+            do_C(i + 2)
             do_M(i + 0)
             do_F(i + -2)
-            do_Q(i + 2)
+            do_Q(i + 1)
             do_L(i + 0)
             do_G(i + -2)
-            do_D(i + 3)
+            do_D(i + 2)
             do_E(i + -1)

@@ -67,14 +67,6 @@ def tile_gatedmemorymodule_pb_t_kernel(tc, queries, memory_items, wq, U_w, W_w, 
         identity = keep.tile([P, P], F32)
         make_identity(nc, identity[:])
 
-        still = keep.tile([P, CHUNK_ROWS], BF16, name="still")
-        nc.vector.memset(still[:], 0.0)
-
-        def stir(times):
-            for i in range(times):
-                unread = sum_banks.tile([P, CHUNK_ROWS], F32, tag="total")
-                nc.tensor.matmul(out=unread[:], lhsT=still[:, 0:P], rhs=still[:], start=True, stop=True)
-
         def load_rows(pool, rows, label, pieces=1):
             raw = pool.tile([P, TILES, FEATURES], BF16, name=label)
             view = rows.rearrange("(p n) k -> p n k", n=TILES)
@@ -346,34 +338,28 @@ def tile_gatedmemorymodule_pb_t_kernel(tc, queries, memory_items, wq, U_w, W_w, 
 
 
         begin_query(0)
-        stir(4)
         turn_all(memory_chunk)
         copy_all(memory_chunk)
         quantise(memory_chunk, 0, 1)
-        stir(1)
         turn_all(pooled_chunk)
         copy_all(pooled_chunk)
         difference(0)
         difference(1)
         quantise(pooled_chunk, 0, 1)
-        stir(1)
         turn_all(u_chunk[0])
         query_raw[2] = load_queries(2)
         copy_all(u_chunk[0])
         difference(2)
         quantise(u_chunk[0], 0, 1)
-        stir(1)
         turn_all(w_chunk[0])
         query_raw[3] = load_queries(3)
         copy_all(w_chunk[0])
         difference(3)
         quantise(w_chunk[0], 0, 1)
-        stir(1)
         turn_all(u_chunk[1])
         query_raw[4] = load_queries(4)
         copy_all(u_chunk[1])
         quantise(u_chunk[1], 0, 1)
-        stir(1)
         turn_all(w_chunk[1])
         query_raw[5] = load_queries(5)
         copy_all(w_chunk[1])

from contextlib import ExitStack

import concourse.mybir as mybir
from concourse.masks import make_identity

F32 = mybir.dt.float32
BF16 = mybir.dt.bfloat16
U32 = mybir.dt.uint32
U8 = mybir.dt.uint8
FP8X4 = mybir.dt.float8_e4m3fn_x4
ACT = mybir.ActivationFunctionType
ALU = mybir.AluOpType

P = 128
FEATURES = 1024
SLOTS = 512
BATCH = 32
TEMPERATURE = 0.1
PACK = 4
K_PASS = P * PACK
PASSES = FEATURES // K_PASS
TILES = 4
CHUNK_ROWS = TILES * P
CHUNK_WORDS = CHUNK_ROWS * PASSES
HALVES = FEATURES // CHUNK_ROWS
QUERY_CHUNKS = BATCH // TILES
ROW_BUFFERS = 6
SORT = {"p": 1, "w0": 1, "u1": 1, "w1": 1}
ROUND = "V"
RG = 4
STORE_TILES = 2

FLOPS = 2 * (2 * SLOTS * FEATURES * FEATURES) + 2 * (P * BATCH) * SLOTS * FEATURES


def stationary_cols(n, g):
    return slice((n * PASSES + g) * P, (n * PASSES + g + 1) * P)


def moving_cols(g):
    return slice(g * CHUNK_ROWS, (g + 1) * CHUNK_ROWS)


def in_tile_order(bank):
    return bank.rearrange("p (n r) -> p r n", n=TILES)


def in_row_order(row):
    return row.rearrange("p (r n) -> p r n", n=TILES)


def tile_gatedmemorymodule_pb_t_kernel(tc, queries, memory_items, wq, U_w, W_w, out_0, out_1):
    nc = tc.nc
    with ExitStack() as ctx:
        keep = ctx.enter_context(tc.tile_pool(name="keep", bufs=1))
        rows_pool = ctx.enter_context(tc.tile_pool(name="rows_pool", bufs=ROW_BUFFERS))
        sorted_pool = ctx.enter_context(tc.tile_pool(name="sorted_pool", bufs=6))
        regroup = ctx.enter_context(tc.tile_pool(name="regroup", bufs=RG))
        mx_pool = ctx.enter_context(tc.tile_pool(name="mx_pool", bufs=7))
        gates = ctx.enter_context(tc.tile_pool(name="gates", bufs=4))
        answers = ctx.enter_context(tc.tile_pool(name="answers", bufs=3))
        stats = ctx.enter_context(tc.tile_pool(name="stats", bufs=3))
        turn_banks = ctx.enter_context(tc.psum_pool(name="turn_banks", bufs=TILES))
        sum_banks = ctx.enter_context(tc.psum_pool(name="sum_banks", bufs=TILES))
        ctx.enter_context(tc.manual_schedule())

        identity = keep.tile([P, P], F32)
        make_identity(nc, identity[:])

        def load_rows(pool, rows, label, pieces=1):
            raw = pool.tile([P, TILES, FEATURES], BF16, name=label)
            view = rows.rearrange("(p n) k -> p n k", n=TILES)
            for i in range(pieces):
                part = slice(i * TILES // pieces, (i + 1) * TILES // pieces)
                nc.sync.dma_start(out=raw[:, part, :], in_=view[:, part, :])
            return raw

        def load_queries(c):
            raw = rows_pool.tile([P, TILES, FEATURES], BF16, name="rows")
            nc.sync.dma_start(out=raw[:], in_=queries[:, c * TILES : (c + 1) * TILES, :])
            return raw

        def new_operand(pool, label):
            codes = pool.tile([P, CHUNK_WORDS], U32, name=label + "_codes", align_bytes=64)
            scales = pool.tile([P, CHUNK_WORDS], U8, name=label + "_scales", align_bytes=64)
            return codes, scales

        def chunk_of(raw, operand, order):
            words = raw[:].bitcast(F32)
            return {
                "raw": words,
                "blocks": [
                    [words[:, n, 2 * P * g + u : 2 * P * (g + 1) : 2] for g in range(PASSES) for u in range(2)]
                    for n in range(TILES)
                ],
                "order": order,
                "operand": operand,
                "banks": {},
            }

        def sort_words(chunk, n, engine_copy):
            ordered = sorted_pool.tile([P, FEATURES], BF16, tag="ordered")
            words = ordered[:].bitcast(F32)
            engine_copy(
                out=words.rearrange("p (g u q) -> p g u q", g=PASSES, u=2),
                in_=chunk["raw"][:, n, :].rearrange("p (g q u) -> p g u q", g=PASSES, u=2),
            )
            chunk["blocks"][n] = [words[:, j * P : (j + 1) * P] for j in range(PACK)]

        def turn(chunk, n, spare=False):
            if spare:
                turned = sum_banks.tile([P, PACK, P], F32, tag="total")
            else:
                turned = turn_banks.tile([P, PACK, P], F32, tag="turned")
            for j in range(PACK):
                nc.tensor.transpose(turned[:, j, :], chunk["blocks"][n][j], identity[:])
            chunk["banks"][n] = turned

        def copy_out(chunk, n, engine_copy):
            if "grouped" not in chunk:
                grouped = regroup.tile([P, CHUNK_WORDS * PACK], BF16, tag="grouped", align_bytes=64)
                chunk["grouped"] = grouped
                chunk["targets"] = grouped[:].bitcast(F32).rearrange(
                    "p (" + chunk["order"] + " u) -> p n g r u", n=TILES, g=PASSES, u=2
                )
            engine_copy(
                out=chunk["targets"][:, n],
                in_=chunk["banks"][n][:].rearrange("p (g u) r -> p g r u", u=2),
            )

        def quantise(chunk, part, parts):
            w = CHUNK_WORDS // parts
            nc.vector.quantize_mx(
                out=chunk["operand"][0][:, part * w : (part + 1) * w].bitcast(FP8X4),
                scales=chunk["operand"][1][:, part * w : (part + 1) * w],
                in_=chunk["grouped"][:, part * w * PACK : (part + 1) * w * PACK],
            )

        def products(total, n, slot_mx, weight_mx, first):
            for g in range(PASSES):
                nc.tensor.matmul_mx(
                    out=total[:],
                    lhsT=slot_mx[0][:, stationary_cols(n, g)].bitcast(FP8X4),
                    lhsT_scale=slot_mx[1][:, stationary_cols(n, g)],
                    rhs=weight_mx[0][:, moving_cols(g)].bitcast(FP8X4),
                    rhs_scale=weight_mx[1][:, moving_cols(g)],
                    start=(first and g == 0),
                    stop=(not first and g == PASSES - 1),
                )

        lifts = {}

        def lift_tile(h, n):
            lift = gates.tile([P, CHUNK_ROWS], F32, tag="lift")
            nc.scalar.activation(out=in_row_order(lift[:]), in_=in_tile_order(sums[h][n][:]), func=ACT.Tanh, scale=0.5)
            lifts[h, n] = lift

        def half_cols(h):
            return slice(h * CHUNK_ROWS, (h + 1) * CHUNK_ROWS)

        def blend_a(h, n):
            nc.vector.scalar_tensor_tensor(
                out=lifts[h, n][:], in0=lifts[h, n][:], scalar=1.0, in1=step[:, n, half_cols(h)], op0=ALU.add, op1=ALU.mult
            )

        def blend_b(h, n):
            nc.vector.scalar_tensor_tensor(
                out=new_slots[:, n, half_cols(h)], in0=lifts[h, n][:], scalar=0.5, in1=memory_raw[:, n, half_cols(h)],
                op0=ALU.mult, op1=ALU.add,
            )

        def round_slots(h, n, engine_copy):
            engine_copy(
                out=rounded[:, n, half_cols(h)].rearrange("p (u q e) -> p u q e", u=2, e=2),
                in_=new_slots[:, n, half_cols(h)].rearrange("p (q u e) -> p u q e", u=2, e=2),
            )

        slot_banks = {}
        slot_grouped = {}

        def turn_slots(h, pair):
            turned = turn_banks.tile([P, PACK, P], F32, tag="turned")
            words = rounded[:].bitcast(F32)
            for i in range(2):
                for u in range(2):
                    lo = h * 2 * P + u * P
                    nc.tensor.transpose(turned[:, 2 * i + u, :], words[:, 2 * pair + i, lo : lo + P], identity[:])
            slot_banks[h, pair] = turned

        def copy_slots(h, pair, engine_copy):
            if h not in slot_grouped:
                grouped = regroup.tile([P, CHUNK_WORDS * PACK], BF16, tag="grouped", align_bytes=64)
                slot_grouped[h] = grouped
            target = slot_grouped[h][:, 0 : SLOTS * PACK].bitcast(F32).rearrange("p (n r u) -> p n r u", n=TILES, u=2)
            engine_copy(
                out=target[:, 2 * pair : 2 * pair + 2],
                in_=slot_banks[h, pair][:].rearrange("p (i u) r -> p i r u", u=2),
            )

        def quantise_slots(h):
            nc.vector.quantize_mx(
                out=new_mx[0][:, moving_cols(h)].bitcast(FP8X4),
                scales=new_mx[1][:, moving_cols(h)],
                in_=slot_grouped[h][:, 0 : SLOTS * PACK],
            )

        def store_slots(h):
            cols = half_cols(h)
            nc.sync.dma_start(
                out=out_0.rearrange("(p n) k -> p n k", n=TILES)[:, :, cols], in_=new_slots[:, :, cols]
            )

        query = {}

        def begin_query(c):
            query[c] = chunk_of(query_raw[c], new_operand(mx_pool, "chunk"), "n g r")

        def begin_answer(c):
            answer = answers.tile([P, TILES, SLOTS], F32)
            shift = stats.tile([P, TILES], F32)
            row_sum = stats.tile([P, TILES], F32)
            inverse = stats.tile([P, TILES], F32)
            query[c]["answer"] = answer
            query[c]["shift"] = shift
            query[c]["row_sum"] = row_sum
            query[c]["inverse"] = inverse
            query[c]["sums"] = {}

        def logit_pass(c, n, g):
            if g == 0:
                total = sum_banks.tile([P, SLOTS], F32, tag="total")
                query[c]["sums"][n] = total
            nc.tensor.matmul_mx(
                out=query[c]["sums"][n][:],
                lhsT=query[c]["operand"][0][:, stationary_cols(n, g)].bitcast(FP8X4),
                lhsT_scale=query[c]["operand"][1][:, stationary_cols(n, g)],
                rhs=new_mx[0][:, moving_cols(g)].bitcast(FP8X4),
                rhs_scale=new_mx[1][:, moving_cols(g)],
                start=(g == 0),
                stop=(g == PASSES - 1),
            )

        def multiply(c, n):
            for g in range(PASSES):
                logit_pass(c, n, g)

        def leave_bank(c, n):
            nc.vector.tensor_scalar(
                out=in_row_order(query[c]["answer"][:, n, :]),
                in0=in_tile_order(query[c]["sums"][n][:]),
                scalar1=-1.0 / TEMPERATURE,
                scalar2=None,
                op0=ALU.mult,
                op1=ALU.min,
                accum_out=query[c]["shift"][:, n : n + 1],
            )

        def exponential(c, n):
            nc.scalar.activation(
                out=query[c]["answer"][:, n, :],
                in_=query[c]["answer"][:, n, :],
                func=ACT.Exp,
                bias=query[c]["shift"][:, n : n + 1],
                scale=-1.0,
                accum_out=query[c]["row_sum"][:, n : n + 1],
            )

        def invert(c, tiles):
            nc.vector.reciprocal(out=query[c]["inverse"][:, tiles], in_=query[c]["row_sum"][:, tiles])

        def normalise(c, n, on_vector):
            row = query[c]["answer"][:, n, :]
            factor = query[c]["inverse"][:, n : n + 1]
            if on_vector:
                nc.vector.tensor_scalar_mul(out=row, in0=row, scalar1=factor)
            else:
                nc.gpsimd.tensor_scalar(out=row, in0=row, scalar1=factor, scalar2=0.0, op0=ALU.mult, op1=ALU.add)

        def store_answer(c, lo, hi):
            nc.sync.dma_start(
                out=out_1[:, c * TILES + lo : c * TILES + hi, :], in_=query[c]["answer"][:, lo:hi, :]
            )

        S = nc.scalar.copy
        V = nc.vector.tensor_copy
        memory_raw = load_rows(keep, memory_items, "memory_raw", 2)
        pooled_raw = load_rows(keep, wq, "pooled_raw", 1)
        u_raw = [load_rows(rows_pool, U_w[0:CHUNK_ROWS, :], "rows", 1)]
        w_raw = [load_rows(rows_pool, W_w[0:CHUNK_ROWS, :], "rows", 1)]
        u_raw.append(load_rows(rows_pool, U_w[CHUNK_ROWS:FEATURES, :], "rows", 2))
        w_raw.append(load_rows(rows_pool, W_w[CHUNK_ROWS:FEATURES, :], "rows", 2))
        query_raw = {}
        for c in range(2):
            query_raw[c] = load_queries(c)

        memory_mx = new_operand(keep, "memory")
        pooled_mx = new_operand(keep, "pooled")
        u_mx = [new_operand(mx_pool, "chunk")]
        w_mx = [new_operand(mx_pool, "chunk")]
        u_mx.append(new_operand(mx_pool, "chunk"))
        w_mx.append(new_operand(mx_pool, "chunk"))
        new_mx = new_operand(keep, "new_slots")
        step = keep.tile([P, TILES, FEATURES], F32)
        new_slots = keep.tile([P, TILES, FEATURES], F32)
        rounded = keep.tile([P, TILES, FEATURES], BF16)

        memory_chunk = chunk_of(memory_raw, memory_mx, "n g r")
        pooled_chunk = chunk_of(pooled_raw, pooled_mx, "n g r")
        u_chunk = [chunk_of(u_raw[h], u_mx[h], "g n r") for h in range(HALVES)]
        w_chunk = [chunk_of(w_raw[h], w_mx[h], "g n r") for h in range(HALVES)]

        def difference(n):
            nc.vector.tensor_sub(out=step[:, n, :], in0=pooled_raw[:, n, :], in1=memory_raw[:, n, :])

        sums = [{}, {}]

        def start_sums(h, tiles):
            for n in tiles:
                total = sum_banks.tile([P, CHUNK_ROWS], F32, tag="total")
                sums[h][n] = total
                products(total, n, memory_mx, u_mx[h], True)

        def finish_sums(h, tiles):
            for n in tiles:
                products(sums[h][n], n, pooled_mx, w_mx[h], False)

        LOW = (0, 1)
        HIGH = (2, 3)
        ALL = (0, 1, 2, 3)

        def turn_all(chunk, tiles=ALL, spare=False):
            for n in tiles:
                turn(chunk, n, spare)

        def copy_all(chunk, tiles=ALL, eng=S):
            for n in tiles:
                copy_out(chunk, n, eng)


        begin_query(0)
        turn_all(memory_chunk)
        copy_all(memory_chunk)
        quantise(memory_chunk, 0, 1)
        turn_all(pooled_chunk)
        copy_all(pooled_chunk)
        difference(0)
        difference(1)
        quantise(pooled_chunk, 0, 1)
        turn_all(u_chunk[0])
        query_raw[2] = load_queries(2)
        copy_all(u_chunk[0])
        difference(2)
        quantise(u_chunk[0], 0, 1)
        turn_all(w_chunk[0])
        query_raw[3] = load_queries(3)
        copy_all(w_chunk[0])
        difference(3)
        quantise(w_chunk[0], 0, 1)
        turn_all(u_chunk[1])
        query_raw[4] = load_queries(4)
        copy_all(u_chunk[1])
        quantise(u_chunk[1], 0, 1)
        turn_all(w_chunk[1])
        query_raw[5] = load_queries(5)
        copy_all(w_chunk[1])
        quantise(w_chunk[1], 0, 1)
        begin_query(1)
        tiles = [(h, n) for h in range(HALVES) for n in range(TILES)]
        for i in range(len(tiles) + 1):
            if i < len(tiles):
                h, n = tiles[i]
                if i == 99:
                    turn_slots(0, 0)
                    turn_slots(0, 1)
                start_sums(h, (n,))
                finish_sums(h, (n,))
                lift_tile(h, n)
                blend_a(h, n)
            if 0 < i:
                blend_b(*tiles[i - 1])
            if 3 <= i < len(tiles):
                round_slots(*tiles[i - 3], S)
        turn_slots(0, 0)
        turn_slots(0, 1)
        turn_all(query[0], ALL, True)
        store_slots(0)
        for i in range(len(tiles) - 3, len(tiles) - 2):
            round_slots(*tiles[i], S)
        copy_slots(0, 0, S)
        copy_slots(0, 1, S)
        copy_all(query[0], LOW)
        for i in range(len(tiles) - 2, len(tiles)):
            round_slots(*tiles[i], V)
        quantise_slots(0)
        turn_slots(1, 0)
        turn_slots(1, 1)
        turn_all(query[1], LOW)
        quantise(query[0], 0, 2)
        copy_slots(1, 0, S)
        copy_slots(1, 1, S)
        copy_all(query[0], HIGH, S)
        quantise_slots(1)
        quantise(query[0], 1, 2)
        store_slots(1)
        begin_answer(0)
        for n in LOW:
            multiply(0, n)
        for n in HIGH:
            multiply(0, n)
        copy_all(query[1], LOW)
        for n in (2, 3):
            sort_words(query[1], n, V)
        quantise(query[1], 0, 2)
        def finish(c, tiles, vec, sharing):
            invert(c, slice(tiles[0], tiles[0] + len(tiles)))
            for k, n in enumerate(tiles):
                if not (sharing and k == 1):
                    normalise(c, n, vec)
            if not sharing:
                store_answer(c, tiles[0], tiles[0] + len(tiles))

        def shares(j):
            return j < 14

        steps = [(c, pair) for c in range(QUERY_CHUNKS) for pair in (LOW, HIGH)]
        NS = len(steps)
        NVEC = ()
        VCOPY = ()
        P0 = 3

        def do_T(j):
            if P0 <= j < NS:
                c, pair = steps[j]
                if pair == LOW and c > 1:
                    begin_query(c)
                turn_all(query[c], pair)
                if pair == HIGH and 6 <= c + 5 < QUERY_CHUNKS:
                    query_raw[c + 5] = load_queries(c + 5)

        def do_C(j):
            if P0 <= j < NS:
                for k, n in enumerate(steps[j][1]):
                    if (j, k) not in VCOPY:
                        copy_out(query[steps[j][0]], n, S)

        def do_D(j):
            if P0 <= j < NS:
                for k, n in enumerate(steps[j][1]):
                    if (j, k) in VCOPY:
                        copy_out(query[steps[j][0]], n, V)

        def do_Q(j):
            if P0 <= j < NS:
                quantise(query[steps[j][0]], steps[j][1][0] // 2, 2)

        def do_M(j):
            if 2 <= j < NS:
                c, pair = steps[j]
                if pair == LOW:
                    begin_answer(c)
                for n in pair:
                    multiply(c, n)

        def do_L(j):
            if 0 <= j < NS:
                for n in steps[j][1]:
                    leave_bank(steps[j][0], n)

        def do_E(j):
            if 0 <= j < NS:
                for n in steps[j][1]:
                    exponential(steps[j][0], n)

        def do_F(j):
            if 0 <= j < NS - 1:
                finish(steps[j][0], steps[j][1], j >= NS - 2, shares(j))
            elif j == NS - 1:
                for n in steps[j][1]:
                    finish(steps[j][0], (n,), True, False)

        def do_G(j):
            if 0 <= j < NS and shares(j):
                c, tiles = steps[j]
                normalise(c, tiles[1], True)
                store_answer(c, tiles[0], tiles[0] + len(tiles))

        for i in range(-3, NS + 4):
            do_T(i + 2)
            do_C(i + 2)
            do_M(i + 0)
            do_F(i + -2)
            do_Q(i + 1)
            do_L(i + 0)
            do_G(i + -2)
            do_D(i + 2)
            do_E(i + -1)
